import numpy as np
import ml_dtypes


def mxq(x, axis, fmt="e4m3"):
    dtype, down = {"e4m3": (ml_dtypes.float8_e4m3fn, 7), "e5m2": (ml_dtypes.float8_e5m2, 14)}[fmt]
    v = np.moveaxis(np.asarray(x, np.float32).astype(ml_dtypes.bfloat16).astype(np.float64), axis, -1)
    blocks = v.reshape(v.shape[:-1] + (-1, 32))
    amax = np.abs(blocks).max(-1, keepdims=True)
    byte = np.maximum(np.where(amax > 0, np.frexp(amax)[1] - 1 + 127, 0) - down, 1)
    scale = np.exp2(byte - 127.0)
    codes = (blocks / scale).astype(np.float32).astype(dtype).astype(np.float64)
    return np.moveaxis((codes * scale).reshape(v.shape), -1, axis)


WIDE = False


def mx_kscale(k):
    if not WIDE:
        return np.ones(k)
    levels = np.array([18, -18])
    if k % 512:
        return np.exp2(np.random.permutation(np.resize(levels, k // 32))).repeat(32)
    a = np.empty((k // 512, 16))
    for p in range(k // 512):
        a[p, :8] = np.random.permutation(np.resize(levels, 8))
        for g in range(8):
            far = levels[np.abs(levels - a[p, g]) >= 10]
            a[p, g + 8] = far[np.random.randint(len(far))]
    return np.exp2(a.ravel()).repeat(32)


BF16 = ml_dtypes.bfloat16


def bf(x):
    return np.asarray(x, np.float32).astype(BF16)


def f64(x):
    return np.asarray(x).astype(np.float64)


N, TQ, TS, C, E = 2, 512, 1024, 1024, 1024
SQRT_HALF = np.sqrt(0.5)


def setup_inputs():
    s = mx_kscale(N * TQ).reshape(N, TQ, 1)
    u = mx_kscale(TS)
    v = mx_kscale(E)
    x0 = bf(np.random.standard_normal((N, TQ, C)))
    te = bf(np.random.standard_normal((N, TQ, E)))
    k0 = bf(np.random.standard_normal((N, E, TS)) * 1.5 / np.sqrt(E))
    v0 = bf(np.random.standard_normal((E, C)) * (0.5 + np.random.random((E, 1))) / np.sqrt(C))
    g0 = bf(1.0 + 0.1 * np.random.standard_normal(E))
    b0 = bf(0.2 * np.random.standard_normal(E))
    g = bf(np.random.standard_normal((N, TQ, TS)) * np.exp2(np.random.randint(-6, 1, (N, TQ, 1))) / s * u)
    v_rnorm = 1.0 / np.sqrt((f64(v0) * f64(v0)).sum(axis=1))
    return {
        "x": bf(f64(x0) * s),
        "target_embedding": te,
        "encoder_keys": bf(f64(k0) * v[:, None] / u),
        "in_proj_v": bf(f64(v0) / v[:, None]),
        "in_proj_g": g0,
        "in_proj_b": b0,
        "v_rnorm": np.asarray(v_rnorm, np.float32),
        "grad_out": g,
    }


def reference(x, target_embedding, encoder_keys, in_proj_v, in_proj_g, in_proj_b, v_rnorm, grad_out):
    vf = f64(in_proj_v)
    r = f64(v_rnorm)
    keys = mxq(f64(encoder_keys), 2, "e4m3")
    dh = mxq(f64(grad_out), 2, "e5m2") @ keys.transpose(0, 2, 1)
    dz1 = (dh * (SQRT_HALF * f64(in_proj_g) * r)).reshape(N * TQ, E)
    dx = mxq(dz1, 1, "e5m2") @ mxq(vf, 0, "e4m3")
    xf = f64(x).reshape(N * TQ, C)
    d = mxq(dz1, 0, "e5m2").T @ mxq(xf, 0, "e4m3")
    dv = d - vf * (r * r)[:, None] * (d * vf).sum(axis=1, keepdims=True)
    return dx.reshape(N, TQ, C), dv

@@ -1,0 +1,459 @@
+from contextlib import ExitStack
+import math
+
+import concourse.mybir as mybir
+from concourse.masks import make_identity
+
+N_BATCH, TQ, TS, C, E = 2, 512, 1024, 1024, 1024
+FLOPS = 3 * 2 * N_BATCH * TQ * 1024 * 1024
+BYTES = 2 * (N_BATCH * TQ * C + N_BATCH * E * TS + E * C + E + N_BATCH * TQ * TS) + 4 * E + 4 * (N_BATCH * TQ * C + E * C)
+
+F32 = mybir.dt.float32
+BF16 = mybir.dt.bfloat16
+U32 = mybir.dt.uint32
+U8 = mybir.dt.uint8
+E4M3 = mybir.dt.float8_e4m3fn_x4
+E5M2 = mybir.dt.float8_e5m2_x4
+MULT = mybir.AluOpType.mult
+ADD = mybir.AluOpType.add
+COPY = mybir.ActivationFunctionType.Copy
+
+P = 128
+SQRT_HALF = math.sqrt(0.5)
+
+
+def tile_attentionlayer_pa_v_kernel(
+    tc, x, target_embedding, encoder_keys, in_proj_v, in_proj_g, in_proj_b, v_rnorm, grad_out, out_0, out_1
+):
+    nc = tc.nc
+    with ExitStack() as ctx:
+        keep = ctx.enter_context(tc.tile_pool(name="keep", bufs=1))
+        raw = ctx.enter_context(tc.tile_pool(name="raw", bufs=1))
+        grp = ctx.enter_context(tc.tile_pool(name="grp", bufs=3))
+        outs = ctx.enter_context(tc.tile_pool(name="outs", bufs=3))
+        psum = ctx.enter_context(tc.psum_pool(name="psum", bufs=1))
+        ctx.enter_context(tc.manual_schedule())
+
+        def bank(b):
+            return psum.tile([P, 512], F32, name="bank", tag=b, bufs=4 if b in "tm" else 1)
+
+        g_raw = {n: raw.tile([P, 4, TS], BF16, name="g_raw", tag="g_raw%d" % n) for n in range(2)}
+        k_raw = {}
+        x_raw = {(n, h): raw.tile([P, 4, 512], BF16, name="x_raw", tag="x_raw%d%d" % (n, h)) for n in range(2) for h in range(2)}
+        v_raw = {G: raw.tile([P, 4, C], BF16, name="v_raw", tag="v_raw%d" % G) for G in range(2)}
+        gain = keep.tile([P, 2, 4], BF16, name="gain")
+        rnorm = keep.tile([P, 2, 4], F32, name="rnorm")
+
+        def load_grad(n, b0, b1):
+            src = grad_out[n, :, :].rearrange("(b p) k -> p b k", p=P)
+            nc.sync.dma_start(out=g_raw[n][:, b0:b1, :], in_=src[:, b0:b1, :])
+
+        def load_keys(s, t0, t1):
+            n, G = s
+            if s not in k_raw:
+                k_raw[s] = raw.tile([P, 4, TS], BF16, name="k_raw", tag="k_raw%d%d" % s)
+            src = encoder_keys[n, 512 * G : 512 * (G + 1), :].rearrange("(m t) k -> m t k", t=4)
+            nc.sync.dma_start(out=k_raw[s][:, t0:t1, :], in_=src[:, t0:t1, :])
+
+        def load_x(n, h):
+            src = x[n, :, :].rearrange("(p j) c -> p j c", j=4)
+            nc.sync.dma_start(out=x_raw[n, h][:], in_=src[:, :, 512 * h : 512 * (h + 1)])
+
+        def load_v(G, c0, c1):
+            src = in_proj_v[512 * G : 512 * (G + 1), :].rearrange("(p j) c -> p j c", j=4)
+            nc.sync.dma_start(out=v_raw[G][:, :, c0:c1], in_=src[:, :, c0:c1])
+
+        S00, S10, S01, S11 = (0, 0), (1, 0), (0, 1), (1, 1)
+        load_grad(0, 0, 1)
+        load_grad(0, 1, 2)
+        load_grad(0, 2, 4)
+        load_keys(S00, 0, 2)
+        nc.scalar.dma_start(out=gain[:], in_=in_proj_g.rearrange("(g p t) -> p g t", g=2, t=4))
+        nc.scalar.dma_start(out=rnorm[:], in_=v_rnorm.rearrange("(g p t) -> p g t", g=2, t=4))
+        load_x(0, 0)
+        load_keys(S00, 2, 4)
+        load_keys(S01, 0, 2)
+        load_keys(S01, 2, 4)
+        load_x(0, 1)
+        load_grad(1, 0, 2)
+        load_grad(1, 2, 4)
+        load_keys(S10, 0, 2)
+        load_keys(S10, 2, 4)
+        load_x(1, 0)
+        load_keys(S11, 0, 2)
+        load_x(1, 1)
+        load_keys(S11, 2, 4)
+        load_v(0, 0, 1024)
+        load_v(1, 0, 1024)
+
+        ident = keep.tile([P, P], F32, name="ident")
+        make_identity(nc, ident[:])
+        dz_scale = keep.tile([P, 2, 4], F32, name="dz_scale")
+        neg_r2 = keep.tile([P, 2, 4], F32, name="neg_r2")
+
+        def make_constants():
+            nc.vector.scalar_tensor_tensor(out=dz_scale[:], in0=gain[:], scalar=SQRT_HALF, in1=rnorm[:], op0=MULT, op1=MULT)
+            nc.vector.scalar_tensor_tensor(out=neg_r2[:], in0=rnorm[:], scalar=-1.0, in1=rnorm[:], op0=MULT, op1=MULT)
+
+        g_grp, g_codes, g_scl = {}, {}, {}
+        k_grp, k_codes, k_scl = {}, {}, {}
+        x_grp, x_codes, x_scl = {}, {}, {}
+        v_grp, v_codes, v_scl = {}, {}, {}
+        dz, zt_grp, zt_codes, zt_scl = {}, {}, {}, {}
+        ze_grp, ze_codes, ze_scl = {}, {}, {}
+        psb = {}
+
+        def copy(eng, out, in_):
+            if eng == "v":
+                nc.vector.tensor_copy(out=out, in_=in_)
+            elif eng == "g":
+                nc.gpsimd.tensor_scalar(out=out, in0=in_, scalar1=1.0, scalar2=0.0, op0=MULT, op1=ADD)
+            else:
+                nc.scalar.copy(out=out, in_=in_)
+
+        def words_of(t2d):
+            return t2d.bitcast(F32)
+
+        def tg(n, bh, g, b):
+            pt = bank(b)
+            psb["g", n, bh, g] = pt
+            for bb in range(2):
+                w = words_of(g_raw[n][:, 2 * bh + bb, :])
+                for u in range(2):
+                    nc.tensor.transpose(
+                        pt[:, 256 * u + 128 * bb : 256 * u + 128 * (bb + 1)], w[:, 256 * g + u : 256 * (g + 1) : 2], ident[:]
+                    )
+
+        def eg(n, bh, g, eng):
+            if n not in g_grp:
+                g_grp[n] = grp.tile([P, 2, 2048], BF16, name="g_grp", tag="g_grp", bufs=1, align_bytes=64)
+            copy(
+                eng,
+                g_grp[n][:, g, 1024 * bh : 1024 * (bh + 1)].bitcast(F32).rearrange("p (c u) -> p c u", u=2),
+                psb["g", n, bh, g][:].rearrange("p (u c) -> p c u", u=2),
+            )
+
+        def qg(n, g):
+            if n not in g_codes:
+                g_codes[n] = keep.tile([P, 2, 512], U32, name="g_codes", tag="g_codes%d" % n, align_bytes=64)
+                g_scl[n] = keep.tile([P, 2, 512], U8, name="g_scl", tag="g_scl%d" % n, align_bytes=64)
+            nc.vector.quantize_mx(out=g_codes[n][:, g, :].bitcast(E5M2), scales=g_scl[n][:, g, :], in_=g_grp[n][:, g, :])
+
+        def tk(s, th, g, b):
+            pt = bank(b)
+            psb["k", s, th, g] = pt
+            for tt in range(2):
+                w = words_of(k_raw[s][:, 2 * th + tt, :])
+                for u in range(2):
+                    nc.tensor.transpose(
+                        pt[:, 256 * u + 128 * tt : 256 * u + 128 * (tt + 1)], w[:, 256 * g + u : 256 * (g + 1) : 2], ident[:]
+                    )
+
+        def ek(s, th, g, eng):
+            if (s, th) not in k_grp:
+                k_grp[s, th] = grp.tile([P, 2048], BF16, name="k_grp", tag="k_grp", bufs=3, align_bytes=64)
+            copy(
+                eng,
+                k_grp[s, th][:, 1024 * g : 1024 * (g + 1)].bitcast(F32).rearrange("p (c u) -> p c u", u=2),
+                psb["k", s, th, g][:].rearrange("p (u c) -> p c u", u=2),
+            )
+
+        def qk(s, th):
+            k_codes[s, th] = grp.tile([P, 512], U32, name="k_codes", tag="k_codes", bufs=4, align_bytes=64)
+            k_scl[s, th] = grp.tile([P, 512], U8, name="k_scl", tag="k_scl", bufs=4, align_bytes=64)
+            nc.vector.quantize_mx(out=k_codes[s, th][:].bitcast(E4M3), scales=k_scl[s, th][:], in_=k_grp[s, th][:])
+
+        def mm(s, t, b):
+            n, G = s
+            th, tt = t // 2, t % 2
+            pt = bank(b)
+            psb["h", s, t] = pt
+            for g in range(2):
+                cols = slice(256 * g + 128 * tt, 256 * g + 128 * (tt + 1))
+                nc.tensor.matmul_mx(
+                    out=pt[:],
+                    lhsT=k_codes[s, th][:, cols].bitcast(E4M3),
+                    lhsT_scale=k_scl[s, th][:, cols],
+                    rhs=g_codes[n][:, g, :].bitcast(E5M2),
+                    rhs_scale=g_scl[n][:, g, :],
+                    start=(g == 0),
+                    stop=(g == 1),
+                )
+
+        def eh(s, t, eng):
+            n, G = s
+            if s not in dz:
+                dz[s] = grp.tile([P, 4, 512], BF16, name="dz", tag="dz", bufs=4, align_bytes=64)
+            out = dz[s][:, t, :].rearrange("p (u q e) -> p u q e", u=2, e=2)
+            in_ = psb["h", s, t][:].rearrange("p (q u e) -> p u q e", u=2, e=2)
+            scale = dz_scale[:, G, t : t + 1]
+            if eng == "v":
+                nc.vector.tensor_scalar(out=out, in0=in_, scalar1=scale, scalar2=None, op0=MULT)
+            else:
+                nc.scalar.activation(out=out, in_=in_, func=COPY, scale=scale)
+
+        def tz(s, th, b):
+            pt = bank(b)
+            psb["z", s, th] = pt
+            for tt in range(2):
+                for u in range(2):
+                    w = words_of(dz[s][:, 2 * th + tt, 256 * u : 256 * (u + 1)])
+                    nc.tensor.transpose(pt[:, 256 * u + 128 * tt : 256 * u + 128 * (tt + 1)], w, ident[:])
+
+        def ez(s, th, eng):
+            if s not in zt_grp:
+                zt_grp[s] = grp.tile([P, 2048], BF16, name="zt_grp", tag="zt_grp", bufs=2, align_bytes=64)
+            copy(
+                eng,
+                zt_grp[s][:, 1024 * th : 1024 * (th + 1)].bitcast(F32).rearrange("p (c u) -> p c u", u=2),
+                psb["z", s, th][:].rearrange("p (u c) -> p c u", u=2),
+            )
+
+        def qz(s):
+            zt_codes[s] = keep.tile([P, 512], U32, name="zt_codes", tag="zt_codes%d%d" % s, align_bytes=64)
+            zt_scl[s] = keep.tile([P, 512], U8, name="zt_scl", tag="zt_scl%d%d" % s, align_bytes=64)
+            nc.vector.quantize_mx(out=zt_codes[s][:].bitcast(E5M2), scales=zt_scl[s][:], in_=zt_grp[s][:])
+
+        def iz(s, u, eng):
+            if s not in ze_grp:
+                ze_grp[s] = grp.tile([P, 2048], BF16, name="ze_grp", tag="ze_grp", bufs=2, align_bytes=64)
+            copy(
+                eng,
+                ze_grp[s][:, 1024 * u : 1024 * (u + 1)].rearrange("p (e q t) -> p e q t", e=2, t=4),
+                dz[s][:, :, 256 * u : 256 * (u + 1)].rearrange("p t (q e) -> p e q t", e=2),
+            )
+
+        def qe(s):
+            ze_codes[s] = keep.tile([P, 512], U32, name="ze_codes", tag="ze_codes%d%d" % s, align_bytes=64)
+            ze_scl[s] = keep.tile([P, 512], U8, name="ze_scl", tag="ze_scl%d%d" % s, align_bytes=64)
+            nc.vector.quantize_mx(out=ze_codes[s][:].bitcast(E5M2), scales=ze_scl[s][:], in_=ze_grp[s][:])
+
+        def interleave(eng, dst, src):
+            copy(eng, dst.rearrange("p (c i j) -> p c j i", i=4, j=4), src.rearrange("p j (c i) -> p c j i", i=4))
+
+        def ix(n, h, eng, parts=(0, 512)):
+            if (n, h) not in x_grp:
+                x_grp[n, h] = grp.tile([P, 2048], BF16, name="x_grp", tag="x_grp", bufs=2, align_bytes=64)
+            a, b = parts
+            interleave(eng, x_grp[n, h][:, 4 * a : 4 * b], x_raw[n, h][:, :, a:b])
+
+        def qx(n, h):
+            if n not in x_codes:
+                x_codes[n] = keep.tile([P, C], U32, name="x_codes", tag="x_codes%d" % n, align_bytes=64)
+                x_scl[n] = keep.tile([P, C], U8, name="x_scl", tag="x_scl%d" % n, align_bytes=64)
+            cols = slice(512 * h, 512 * (h + 1))
+            nc.vector.quantize_mx(out=x_codes[n][:, cols].bitcast(E4M3), scales=x_scl[n][:, cols], in_=x_grp[n, h][:])
+
+        def iv(G, h, eng, parts=(0, 512)):
+            if (G, h) not in v_grp:
+                v_grp[G, h] = grp.tile([P, 2048], BF16, name="v_grp", tag="v_grp", bufs=2, align_bytes=64)
+            a, b = parts
+            interleave(eng, v_grp[G, h][:, 4 * a : 4 * b], v_raw[G][:, :, 512 * h + a : 512 * h + b])
+
+        def qv(G, h):
+            if G not in v_codes:
+                v_codes[G] = keep.tile([P, C], U32, name="v_codes", tag="v_codes%d" % G, align_bytes=64)
+                v_scl[G] = keep.tile([P, C], U8, name="v_scl", tag="v_scl%d" % G, align_bytes=64)
+            cols = slice(512 * h, 512 * (h + 1))
+            nc.vector.quantize_mx(out=v_codes[G][:, cols].bitcast(E4M3), scales=v_scl[G][:, cols], in_=v_grp[G, h][:])
+
+        def d(G, t, ch, b):
+            pt = bank(b)
+            psb["d", G, t, ch] = pt
+            rows = slice(128 * t, 128 * (t + 1))
+            cols = slice(512 * ch, 512 * (ch + 1))
+            for n in range(2):
+                nc.tensor.matmul_mx(
+                    out=pt[:],
+                    lhsT=zt_codes[n, G][:, rows].bitcast(E5M2),
+                    lhsT_scale=zt_scl[n, G][:, rows],
+                    rhs=x_codes[n][:, cols].bitcast(E4M3),
+                    rhs_scale=x_scl[n][:, cols],
+                    start=(n == 0),
+                    stop=(n == 1),
+                )
+
+        dv, acc, coef = {}, {}, {}
+
+        def fa(G, t, ch):
+            if (G, t) not in dv:
+                dv[G, t] = outs.tile([P, C], F32, name="dv", tag="dv", bufs=4)
+                acc[G, t] = grp.tile([P, 2], F32, name="acc", tag="acc", bufs=3)
+            cols = slice(512 * ch, 512 * (ch + 1))
+            nc.vector.scalar_tensor_tensor(
+                out=dv[G, t][:, cols],
+                in0=psb["d", G, t, ch][:],
+                scalar=1.0,
+                in1=v_raw[G][:, t, cols],
+                op0=MULT,
+                op1=MULT,
+                accum_out=acc[G, t][:, ch : ch + 1],
+            )
+
+        def fc(G, t):
+            coef[G, t] = grp.tile([P, 1], F32, name="coef", tag="coef", bufs=3)
+            nc.vector.tensor_scalar(
+                out=coef[G, t][:],
+                in0=acc[G, t][:, 0:1],
+                scalar1=acc[G, t][:, 1:2],
+                scalar2=neg_r2[:, G, t : t + 1],
+                op0=ADD,
+                op1=MULT,
+            )
+
+        def fb(G, t, ch):
+            cols = slice(512 * ch, 512 * (ch + 1))
+            nc.vector.scalar_tensor_tensor(
+                out=dv[G, t][:, cols],
+                in0=v_raw[G][:, t, cols],
+                scalar=coef[G, t][:],
+                in1=psb["d", G, t, ch][:],
+                op0=MULT,
+                op1=ADD,
+            )
+
+        def store_d(G, t, c0=0, c1=C):
+            dst = out_1[512 * G : 512 * (G + 1), :].rearrange("(p j) c -> p j c", j=4)
+            nc.sync.dma_start(out=dst[:, t, c0:c1], in_=dv[G, t][:, c0:c1])
+
+        ox = {}
+
+        def dx(n, j, ch, b):
+            pt = bank(b)
+            psb["x", n, j, ch] = pt
+            rows = slice(128 * j, 128 * (j + 1))
+            cols = slice(512 * ch, 512 * (ch + 1))
+            for G in range(2):
+                nc.tensor.matmul_mx(
+                    out=pt[:],
+                    lhsT=ze_codes[n, G][:, rows].bitcast(E5M2),
+                    lhsT_scale=ze_scl[n, G][:, rows],
+                    rhs=v_codes[G][:, cols].bitcast(E4M3),
+                    rhs_scale=v_scl[G][:, cols],
+                    start=(G == 0),
+                    stop=(G == 1),
+                )
+
+        def ex(n, j, ch, eng):
+            ox[n, j, ch] = outs.tile([P, 512], F32, name="ox", tag="ox", bufs=4)
+            copy(eng, ox[n, j, ch][:], psb["x", n, j, ch][:])
+
+        def store_x(n, j, ch):
+            dst = out_0[n, :, :].rearrange("(q j) c -> q j c", j=4)
+            nc.sync.dma_start(out=dst[:, j, 512 * ch : 512 * (ch + 1)], in_=ox[n, j, ch][:])
+
+        def dx_half(i, ch):
+            dx(XT[i][0], XT[i][1], ch, "t")
+            ex(XT[i][0], XT[i][1], ch, "s")
+            if (i, ch) != (0, 0):
+                store_x(XT[(i - 1) % 8][0], XT[(i - 1) % 8][1], ch if i > 0 else 0)
+
+        TILES = [(G, t) for G in range(2) for t in range(4)]
+        XT = [(n, j) for n in range(2) for j in range(4)]
+        STEPS = [S00, S01, S10, S11]
+        X_HALF = [(0, 0), (0, 1), (1, 0), (1, 1)]
+
+        def pair_tk(s, th):
+            tk(s, th, 0, "t")
+            tk(s, th, 1, "t")
+            ek(s, th, 0, "s")
+            ek(s, th, 1, "s")
+
+        def pair_mm(s, a):
+            mm(s, a, "m")
+            mm(s, a + 1, "m")
+            eh(s, a, "s")
+            eh(s, a + 1, "s")
+
+        def pair_tg(n, bh, e0, e1):
+            tg(n, bh, 0, "t")
+            tg(n, bh, 1, "t")
+            eg(n, bh, 0, e0)
+            eg(n, bh, 1, e1)
+
+        def pair_tz(s):
+            tz(s, 0, "t")
+            tz(s, 1, "t")
+            ez(s, 0, "s")
+            ez(s, 1, "s")
+
+        make_constants()
+        pair_tg(0, 0, "s", "v")
+        pair_tg(0, 1, "s", "v")
+        qg(0, 0)
+        qg(0, 1)
+        pair_tk(S00, 0)
+        qk(S00, 0)
+        ix(0, 0, "v")
+        pair_tk(S00, 1)
+        qk(S00, 1)
+        qx(0, 0)
+        for k in range(4):
+            s = STEPS[k]
+            if k < 3:
+                pair_tk(STEPS[k + 1], 0)
+                qk(STEPS[k + 1], 0)
+            if k > 0:
+                pair_tz(STEPS[k - 1])
+                iz(STEPS[k - 1], 0, "v")
+                iz(STEPS[k - 1], 1, "v")
+                qz(STEPS[k - 1])
+                qe(STEPS[k - 1])
+            if k == 1:
+                pair_tg(1, 0, "s", "v")
+            pair_mm(s, 0)
+            if k < 3:
+                ix(X_HALF[k + 1][0], X_HALF[k + 1][1], "v")
+                pair_tk(STEPS[k + 1], 1)
+                qk(STEPS[k + 1], 1)
+                qx(X_HALF[k + 1][0], X_HALF[k + 1][1])
+            if k == 1:
+                pair_tg(1, 1, "s", "v")
+                qg(1, 0)
+                qg(1, 1)
+            if k == 3:
+                iv(0, 0, "s", (0, 256))
+            pair_mm(s, 2)
+
+        d(0, 0, 0, "m")
+        d(0, 0, 1, "m")
+        pair_tz(S11)
+        d(0, 1, 0, "m")
+        fa(0, 0, 0)
+        fa(0, 0, 1)
+        iz(S11, 0, "v")
+        fc(0, 0)
+        iz(S11, 1, "v")
+        iv(0, 0, "s", (256, 512))
+        iv(1, 0, "s")
+        qz(S11)
+        qe(S11)
+        qv(0, 0)
+        iv(0, 1, "s")
+        XQ = {1: [(0, 0), (1, 0)], 2: [(2, 0), (3, 0), (4, 0)], 3: [(5, 0), (6, 0), (7, 0)], 4: [(0, 1), (1, 1), (2, 1)], 5: [(3, 1), (4, 1), (5, 1)], 6: [(6, 1), (7, 1)]}
+        for i in range(8):
+            G, t = TILES[i]
+            if i < 7:
+                G1, t1 = TILES[i + 1]
+                fa(G1, t1, 0)
+                if i == 1:
+                    qv(1, 0)
+                if i == 2:
+                    qv(0, 1)
+                if i == 4:
+                    qv(1, 1)
+            fb(G, t, 0)
+            if i < 7:
+                d(G1, t1, 1, "m")
+                fa(G1, t1, 1)
+            fb(G, t, 1)
+            store_d(G, t)
+            if i < 6:
+                d(TILES[i + 2][0], TILES[i + 2][1], 0, "m")
+            if i < 7:
+                fc(G1, t1)
+            for q in XQ.get(i, []):
+                dx_half(q[0], q[1])
+            if i == 2:
+                iv(1, 1, "s")
+        store_x(1, 3, 1)

@@ -4,9 +4,11 @@ import math
 import concourse.mybir as mybir
 from concourse.masks import make_identity
 
-N_BATCH, TQ, TS, C, E = 2, 512, 1024, 1024, 1024
-FLOPS = 3 * 2 * N_BATCH * TQ * 1024 * 1024
-BYTES = 2 * (N_BATCH * TQ * C + N_BATCH * E * TS + E * C + E + N_BATCH * TQ * TS) + 4 * E + 4 * (N_BATCH * TQ * C + E * C)
+N, TQ, TS, C, E = 2, 512, 1024, 1024, 1024
+TOKENS = N * TQ
+
+FLOPS = 2 * TOKENS * (TS * E + E * C + E * C)
+BYTES = 2 * (N * TQ * C + N * E * TS + E * C + E + N * TQ * TS) + 4 * E + 4 * (TOKENS * C + E * C)
 
 F32 = mybir.dt.float32
 BF16 = mybir.dt.bfloat16
@@ -19,441 +21,457 @@ ADD = mybir.AluOpType.add
 COPY = mybir.ActivationFunctionType.Copy
 
 P = 128
+BANK = 512
 SQRT_HALF = math.sqrt(0.5)
+
+S00, S01, S10, S11 = (0, 0), (0, 1), (1, 0), (1, 1)
 
 
 def tile_attentionlayer_pa_v_kernel(
     tc, x, target_embedding, encoder_keys, in_proj_v, in_proj_g, in_proj_b, v_rnorm, grad_out, out_0, out_1
 ):
     nc = tc.nc
+
     with ExitStack() as ctx:
-        keep = ctx.enter_context(tc.tile_pool(name="keep", bufs=1))
         raw = ctx.enter_context(tc.tile_pool(name="raw", bufs=1))
-        grp = ctx.enter_context(tc.tile_pool(name="grp", bufs=3))
-        outs = ctx.enter_context(tc.tile_pool(name="outs", bufs=3))
+        work = ctx.enter_context(tc.tile_pool(name="work", bufs=2))
+        keep = ctx.enter_context(tc.tile_pool(name="keep", bufs=1))
         psum = ctx.enter_context(tc.psum_pool(name="psum", bufs=1))
         ctx.enter_context(tc.manual_schedule())
 
-        def bank(b):
-            return psum.tile([P, 512], F32, name="bank", tag=b, bufs=4 if b in "tm" else 1)
+        free_banks = list(range(8))
+        banks = {}
 
-        g_raw = {n: raw.tile([P, 4, TS], BF16, name="g_raw", tag="g_raw%d" % n) for n in range(2)}
-        k_raw = {}
-        x_raw = {(n, h): raw.tile([P, 4, 512], BF16, name="x_raw", tag="x_raw%d%d" % (n, h)) for n in range(2) for h in range(2)}
-        v_raw = {G: raw.tile([P, 4, C], BF16, name="v_raw", tag="v_raw%d" % G) for G in range(2)}
+        def take_bank(key):
+            b = free_banks[0]
+            free_banks.remove(b)
+            banks[key] = (b, psum.tile([P, BANK], F32, name="bank", tag="bank%d" % b))
+            return banks[key][1]
+
+        def bank_of(key):
+            return banks[key][1]
+
+        def give_bank(key):
+            free_banks.append(banks[key][0])
+
+        def copy_on(engine, out, in_):
+            if engine == "V":
+                nc.vector.tensor_copy(out=out, in_=in_)
+            else:
+                nc.scalar.copy(out=out, in_=in_)
+
+        grad_raw = {n: raw.tile([P, 4, TS], BF16, name="grad_raw", tag="grad%d" % n) for n in range(N)}
+        keys_raw = {s: raw.tile([P, 4, TS], BF16, name="keys_raw", tag="keys%d%d" % s) for s in (S00, S01, S10, S11)}
+        x_raw = {s: raw.tile([P, 4, BANK], BF16, name="x_raw", tag="x%d%d" % s) for s in (S00, S01, S10, S11)}
+        v_raw = {h: raw.tile([P, 4, C], BF16, name="v_raw", tag="v%d" % h) for h in range(2)}
         gain = keep.tile([P, 2, 4], BF16, name="gain")
         rnorm = keep.tile([P, 2, 4], F32, name="rnorm")
 
-        def load_grad(n, b0, b1):
-            src = grad_out[n, :, :].rearrange("(b p) k -> p b k", p=P)
-            nc.sync.dma_start(out=g_raw[n][:, b0:b1, :], in_=src[:, b0:b1, :])
+        def load_grad(n, b):
+            src = grad_out[n, :, :].rearrange("(p j) k -> p j k", j=4)
+            nc.sync.dma_start(out=grad_raw[n][:, 2 * b : 2 * b + 2, :], in_=src[:, 2 * b : 2 * b + 2, :])
 
-        def load_keys(s, t0, t1):
-            n, G = s
-            if s not in k_raw:
-                k_raw[s] = raw.tile([P, 4, TS], BF16, name="k_raw", tag="k_raw%d%d" % s)
-            src = encoder_keys[n, 512 * G : 512 * (G + 1), :].rearrange("(m t) k -> m t k", t=4)
-            nc.sync.dma_start(out=k_raw[s][:, t0:t1, :], in_=src[:, t0:t1, :])
+        def load_keys(step, b):
+            n, h = step
+            src = encoder_keys[n, 512 * h : 512 * (h + 1), :].rearrange("(p j) k -> p j k", j=4)
+            nc.sync.dma_start(out=keys_raw[step][:, 2 * b : 2 * b + 2, :], in_=src[:, 2 * b : 2 * b + 2, :])
 
-        def load_x(n, h):
+        def load_x(n, ch):
             src = x[n, :, :].rearrange("(p j) c -> p j c", j=4)
-            nc.sync.dma_start(out=x_raw[n, h][:], in_=src[:, :, 512 * h : 512 * (h + 1)])
+            nc.sync.dma_start(out=x_raw[n, ch][:], in_=src[:, :, BANK * ch : BANK * (ch + 1)])
 
-        def load_v(G, c0, c1):
-            src = in_proj_v[512 * G : 512 * (G + 1), :].rearrange("(p j) c -> p j c", j=4)
-            nc.sync.dma_start(out=v_raw[G][:, :, c0:c1], in_=src[:, :, c0:c1])
+        def load_v(h):
+            nc.sync.dma_start(
+                out=v_raw[h][:], in_=in_proj_v[512 * h : 512 * (h + 1), :].rearrange("(p j) c -> p j c", j=4)
+            )
 
-        S00, S10, S01, S11 = (0, 0), (1, 0), (0, 1), (1, 1)
-        load_grad(0, 0, 1)
-        load_grad(0, 1, 2)
-        load_grad(0, 2, 4)
-        load_keys(S00, 0, 2)
-        nc.scalar.dma_start(out=gain[:], in_=in_proj_g.rearrange("(g p t) -> p g t", g=2, t=4))
-        nc.scalar.dma_start(out=rnorm[:], in_=v_rnorm.rearrange("(g p t) -> p g t", g=2, t=4))
-        load_x(0, 0)
-        load_keys(S00, 2, 4)
-        load_keys(S01, 0, 2)
-        load_keys(S01, 2, 4)
-        load_x(0, 1)
-        load_grad(1, 0, 2)
-        load_grad(1, 2, 4)
-        load_keys(S10, 0, 2)
-        load_keys(S10, 2, 4)
+        def load_vectors():
+            nc.sync.dma_start(out=gain[:], in_=in_proj_g.rearrange("(h p j) -> p h j", h=2, j=4))
+            nc.sync.dma_start(out=rnorm[:], in_=v_rnorm.rearrange("(h p j) -> p h j", h=2, j=4))
+
+        load_grad(0, 0)
+        load_grad(1, 0)
+        load_keys(S00, 0)
+        load_grad(1, 1)
+        load_grad(0, 1)
         load_x(1, 0)
-        load_keys(S11, 0, 2)
+        load_vectors()
+        load_keys(S01, 0)
+        load_keys(S00, 1)
+        load_v(0)
+        load_keys(S10, 0)
+        load_x(0, 0)
+        load_keys(S10, 1)
+        load_x(0, 1)
+        load_keys(S01, 1)
         load_x(1, 1)
-        load_keys(S11, 2, 4)
-        load_v(0, 0, 1024)
-        load_v(1, 0, 1024)
+        load_v(1)
+        load_keys(S11, 0)
+        load_keys(S11, 1)
 
         ident = keep.tile([P, P], F32, name="ident")
         make_identity(nc, ident[:])
         dz_scale = keep.tile([P, 2, 4], F32, name="dz_scale")
-        neg_r2 = keep.tile([P, 2, 4], F32, name="neg_r2")
+        minus_r2 = keep.tile([P, 2, 4], F32, name="minus_r2")
 
-        def make_constants():
-            nc.vector.scalar_tensor_tensor(out=dz_scale[:], in0=gain[:], scalar=SQRT_HALF, in1=rnorm[:], op0=MULT, op1=MULT)
-            nc.vector.scalar_tensor_tensor(out=neg_r2[:], in0=rnorm[:], scalar=-1.0, in1=rnorm[:], op0=MULT, op1=MULT)
-
-        g_grp, g_codes, g_scl = {}, {}, {}
-        k_grp, k_codes, k_scl = {}, {}, {}
-        x_grp, x_codes, x_scl = {}, {}, {}
-        v_grp, v_codes, v_scl = {}, {}, {}
-        dz, zt_grp, zt_codes, zt_scl = {}, {}, {}, {}
-        ze_grp, ze_codes, ze_scl = {}, {}, {}
-        psb = {}
-
-        def copy(eng, out, in_):
-            if eng == "v":
-                nc.vector.tensor_copy(out=out, in_=in_)
-            elif eng == "g":
-                nc.gpsimd.tensor_scalar(out=out, in0=in_, scalar1=1.0, scalar2=0.0, op0=MULT, op1=ADD)
-            else:
-                nc.scalar.copy(out=out, in_=in_)
-
-        def words_of(t2d):
-            return t2d.bitcast(F32)
-
-        def tg(n, bh, g, b):
-            pt = bank(b)
-            psb["g", n, bh, g] = pt
-            for bb in range(2):
-                w = words_of(g_raw[n][:, 2 * bh + bb, :])
-                for u in range(2):
-                    nc.tensor.transpose(
-                        pt[:, 256 * u + 128 * bb : 256 * u + 128 * (bb + 1)], w[:, 256 * g + u : 256 * (g + 1) : 2], ident[:]
-                    )
-
-        def eg(n, bh, g, eng):
-            if n not in g_grp:
-                g_grp[n] = grp.tile([P, 2, 2048], BF16, name="g_grp", tag="g_grp", bufs=1, align_bytes=64)
-            copy(
-                eng,
-                g_grp[n][:, g, 1024 * bh : 1024 * (bh + 1)].bitcast(F32).rearrange("p (c u) -> p c u", u=2),
-                psb["g", n, bh, g][:].rearrange("p (u c) -> p c u", u=2),
-            )
-
-        def qg(n, g):
-            if n not in g_codes:
-                g_codes[n] = keep.tile([P, 2, 512], U32, name="g_codes", tag="g_codes%d" % n, align_bytes=64)
-                g_scl[n] = keep.tile([P, 2, 512], U8, name="g_scl", tag="g_scl%d" % n, align_bytes=64)
-            nc.vector.quantize_mx(out=g_codes[n][:, g, :].bitcast(E5M2), scales=g_scl[n][:, g, :], in_=g_grp[n][:, g, :])
-
-        def tk(s, th, g, b):
-            pt = bank(b)
-            psb["k", s, th, g] = pt
-            for tt in range(2):
-                w = words_of(k_raw[s][:, 2 * th + tt, :])
-                for u in range(2):
-                    nc.tensor.transpose(
-                        pt[:, 256 * u + 128 * tt : 256 * u + 128 * (tt + 1)], w[:, 256 * g + u : 256 * (g + 1) : 2], ident[:]
-                    )
-
-        def ek(s, th, g, eng):
-            if (s, th) not in k_grp:
-                k_grp[s, th] = grp.tile([P, 2048], BF16, name="k_grp", tag="k_grp", bufs=3, align_bytes=64)
-            copy(
-                eng,
-                k_grp[s, th][:, 1024 * g : 1024 * (g + 1)].bitcast(F32).rearrange("p (c u) -> p c u", u=2),
-                psb["k", s, th, g][:].rearrange("p (u c) -> p c u", u=2),
-            )
-
-        def qk(s, th):
-            k_codes[s, th] = grp.tile([P, 512], U32, name="k_codes", tag="k_codes", bufs=4, align_bytes=64)
-            k_scl[s, th] = grp.tile([P, 512], U8, name="k_scl", tag="k_scl", bufs=4, align_bytes=64)
-            nc.vector.quantize_mx(out=k_codes[s, th][:].bitcast(E4M3), scales=k_scl[s, th][:], in_=k_grp[s, th][:])
-
-        def mm(s, t, b):
-            n, G = s
-            th, tt = t // 2, t % 2
-            pt = bank(b)
-            psb["h", s, t] = pt
-            for g in range(2):
-                cols = slice(256 * g + 128 * tt, 256 * g + 128 * (tt + 1))
-                nc.tensor.matmul_mx(
-                    out=pt[:],
-                    lhsT=k_codes[s, th][:, cols].bitcast(E4M3),
-                    lhsT_scale=k_scl[s, th][:, cols],
-                    rhs=g_codes[n][:, g, :].bitcast(E5M2),
-                    rhs_scale=g_scl[n][:, g, :],
-                    start=(g == 0),
-                    stop=(g == 1),
-                )
-
-        def eh(s, t, eng):
-            n, G = s
-            if s not in dz:
-                dz[s] = grp.tile([P, 4, 512], BF16, name="dz", tag="dz", bufs=4, align_bytes=64)
-            out = dz[s][:, t, :].rearrange("p (u q e) -> p u q e", u=2, e=2)
-            in_ = psb["h", s, t][:].rearrange("p (q u e) -> p u q e", u=2, e=2)
-            scale = dz_scale[:, G, t : t + 1]
-            if eng == "v":
-                nc.vector.tensor_scalar(out=out, in0=in_, scalar1=scale, scalar2=None, op0=MULT)
-            else:
-                nc.scalar.activation(out=out, in_=in_, func=COPY, scale=scale)
-
-        def tz(s, th, b):
-            pt = bank(b)
-            psb["z", s, th] = pt
-            for tt in range(2):
-                for u in range(2):
-                    w = words_of(dz[s][:, 2 * th + tt, 256 * u : 256 * (u + 1)])
-                    nc.tensor.transpose(pt[:, 256 * u + 128 * tt : 256 * u + 128 * (tt + 1)], w, ident[:])
-
-        def ez(s, th, eng):
-            if s not in zt_grp:
-                zt_grp[s] = grp.tile([P, 2048], BF16, name="zt_grp", tag="zt_grp", bufs=2, align_bytes=64)
-            copy(
-                eng,
-                zt_grp[s][:, 1024 * th : 1024 * (th + 1)].bitcast(F32).rearrange("p (c u) -> p c u", u=2),
-                psb["z", s, th][:].rearrange("p (u c) -> p c u", u=2),
-            )
-
-        def qz(s):
-            zt_codes[s] = keep.tile([P, 512], U32, name="zt_codes", tag="zt_codes%d%d" % s, align_bytes=64)
-            zt_scl[s] = keep.tile([P, 512], U8, name="zt_scl", tag="zt_scl%d%d" % s, align_bytes=64)
-            nc.vector.quantize_mx(out=zt_codes[s][:].bitcast(E5M2), scales=zt_scl[s][:], in_=zt_grp[s][:])
-
-        def iz(s, u, eng):
-            if s not in ze_grp:
-                ze_grp[s] = grp.tile([P, 2048], BF16, name="ze_grp", tag="ze_grp", bufs=2, align_bytes=64)
-            copy(
-                eng,
-                ze_grp[s][:, 1024 * u : 1024 * (u + 1)].rearrange("p (e q t) -> p e q t", e=2, t=4),
-                dz[s][:, :, 256 * u : 256 * (u + 1)].rearrange("p t (q e) -> p e q t", e=2),
-            )
-
-        def qe(s):
-            ze_codes[s] = keep.tile([P, 512], U32, name="ze_codes", tag="ze_codes%d%d" % s, align_bytes=64)
-            ze_scl[s] = keep.tile([P, 512], U8, name="ze_scl", tag="ze_scl%d%d" % s, align_bytes=64)
-            nc.vector.quantize_mx(out=ze_codes[s][:].bitcast(E5M2), scales=ze_scl[s][:], in_=ze_grp[s][:])
-
-        def interleave(eng, dst, src):
-            copy(eng, dst.rearrange("p (c i j) -> p c j i", i=4, j=4), src.rearrange("p j (c i) -> p c j i", i=4))
-
-        def ix(n, h, eng, parts=(0, 512)):
-            if (n, h) not in x_grp:
-                x_grp[n, h] = grp.tile([P, 2048], BF16, name="x_grp", tag="x_grp", bufs=2, align_bytes=64)
-            a, b = parts
-            interleave(eng, x_grp[n, h][:, 4 * a : 4 * b], x_raw[n, h][:, :, a:b])
-
-        def qx(n, h):
-            if n not in x_codes:
-                x_codes[n] = keep.tile([P, C], U32, name="x_codes", tag="x_codes%d" % n, align_bytes=64)
-                x_scl[n] = keep.tile([P, C], U8, name="x_scl", tag="x_scl%d" % n, align_bytes=64)
-            cols = slice(512 * h, 512 * (h + 1))
-            nc.vector.quantize_mx(out=x_codes[n][:, cols].bitcast(E4M3), scales=x_scl[n][:, cols], in_=x_grp[n, h][:])
-
-        def iv(G, h, eng, parts=(0, 512)):
-            if (G, h) not in v_grp:
-                v_grp[G, h] = grp.tile([P, 2048], BF16, name="v_grp", tag="v_grp", bufs=2, align_bytes=64)
-            a, b = parts
-            interleave(eng, v_grp[G, h][:, 4 * a : 4 * b], v_raw[G][:, :, 512 * h + a : 512 * h + b])
-
-        def qv(G, h):
-            if G not in v_codes:
-                v_codes[G] = keep.tile([P, C], U32, name="v_codes", tag="v_codes%d" % G, align_bytes=64)
-                v_scl[G] = keep.tile([P, C], U8, name="v_scl", tag="v_scl%d" % G, align_bytes=64)
-            cols = slice(512 * h, 512 * (h + 1))
-            nc.vector.quantize_mx(out=v_codes[G][:, cols].bitcast(E4M3), scales=v_scl[G][:, cols], in_=v_grp[G, h][:])
-
-        def d(G, t, ch, b):
-            pt = bank(b)
-            psb["d", G, t, ch] = pt
-            rows = slice(128 * t, 128 * (t + 1))
-            cols = slice(512 * ch, 512 * (ch + 1))
-            for n in range(2):
-                nc.tensor.matmul_mx(
-                    out=pt[:],
-                    lhsT=zt_codes[n, G][:, rows].bitcast(E5M2),
-                    lhsT_scale=zt_scl[n, G][:, rows],
-                    rhs=x_codes[n][:, cols].bitcast(E4M3),
-                    rhs_scale=x_scl[n][:, cols],
-                    start=(n == 0),
-                    stop=(n == 1),
-                )
-
-        dv, acc, coef = {}, {}, {}
-
-        def fa(G, t, ch):
-            if (G, t) not in dv:
-                dv[G, t] = outs.tile([P, C], F32, name="dv", tag="dv", bufs=4)
-                acc[G, t] = grp.tile([P, 2], F32, name="acc", tag="acc", bufs=3)
-            cols = slice(512 * ch, 512 * (ch + 1))
+        def make_factors():
             nc.vector.scalar_tensor_tensor(
-                out=dv[G, t][:, cols],
-                in0=psb["d", G, t, ch][:],
-                scalar=1.0,
-                in1=v_raw[G][:, t, cols],
-                op0=MULT,
-                op1=MULT,
-                accum_out=acc[G, t][:, ch : ch + 1],
+                out=dz_scale[:], in0=gain[:], scalar=SQRT_HALF, in1=rnorm[:], op0=MULT, op1=MULT
+            )
+            nc.vector.scalar_tensor_tensor(
+                out=minus_r2[:], in0=rnorm[:], scalar=-1.0, in1=rnorm[:], op0=MULT, op1=MULT
             )
 
-        def fc(G, t):
-            coef[G, t] = grp.tile([P, 1], F32, name="coef", tag="coef", bufs=3)
+        def codes_and_scales(pool, width, name, tag, bufs):
+            codes = pool.tile([P, width], U32, name=name, tag=tag, bufs=bufs, align_bytes=64)
+            scales = pool.tile([P, width], U8, name=name + "_scales", tag=tag + "_scales", bufs=bufs, align_bytes=64)
+            return codes, scales
+
+        def quantize(codes, scales, cols, in_, fmt):
+            nc.vector.quantize_mx(out=codes[:, cols].bitcast(fmt), scales=scales[:, cols], in_=in_)
+
+        def transpose_words(key, row_tiles, runs):
+            pt = take_bank(key)
+            for i in range(2):
+                words = row_tiles[i].bitcast(F32)
+                for u in range(2):
+                    nc.tensor.transpose(
+                        pt[:, 256 * u + 128 * i : 256 * u + 128 * (i + 1)], words[:, runs[u]], ident[:]
+                    )
+
+        def copy_words(key, out, engine):
+            copy_on(
+                engine,
+                out.bitcast(F32).rearrange("p (r u) -> p r u", u=2),
+                bank_of(key)[:].rearrange("p (u r) -> p r u", u=2),
+            )
+            give_bank(key)
+
+        def position_runs(g):
+            return [slice(256 * g + u, 256 * (g + 1), 2) for u in range(2)]
+
+        grad_side, grad_codes = {}, {}
+
+        def transpose_grad(n, b, engines):
+            for g in range(2):
+                transpose_words(("grad", n, b, g), [grad_raw[n][:, 2 * b + i, :] for i in range(2)], position_runs(g))
+            if n not in grad_side:
+                grad_side[n] = work.tile([P, 2, 4 * BANK], BF16, name="grad_side", tag="grad_side", align_bytes=64)
+            for g in range(2):
+                copy_words(("grad", n, b, g), grad_side[n][:, g, 1024 * b : 1024 * (b + 1)], engines[g])
+
+        def quantize_grad(n, g):
+            if n not in grad_codes:
+                grad_codes[n] = codes_and_scales(keep, 2 * BANK, "grad_codes", "grad_codes%d" % n, 1)
+            quantize(*grad_codes[n], slice(BANK * g, BANK * (g + 1)), grad_side[n][:, g, :], E5M2)
+
+        keys_side, keys_codes = {}, {}
+
+        def transpose_keys(step, b, engines):
+            for g in range(2):
+                transpose_words(
+                    ("keys", step, b, g), [keys_raw[step][:, 2 * b + i, :] for i in range(2)], position_runs(g)
+                )
+            keys_side[step, b] = work.tile([P, 4 * BANK], BF16, name="keys_side", tag="keys_side", bufs=4, align_bytes=64)
+            for g in range(2):
+                copy_words(("keys", step, b, g), keys_side[step, b][:, 1024 * g : 1024 * (g + 1)], engines[g])
+
+        def quantize_keys(step, b):
+            keys_codes[step, b] = codes_and_scales(work, BANK, "keys_codes", "keys_codes", 6)
+            quantize(*keys_codes[step, b], slice(0, BANK), keys_side[step, b][:], E4M3)
+
+        x_side, x_codes, v_side, v_codes = {}, {}, {}, {}
+
+        def interleave_x(n, ch, engine):
+            x_side[n, ch] = work.tile([P, 4 * BANK], BF16, name="x_side", tag="x_side", align_bytes=64)
+            copy_on(
+                engine,
+                x_side[n, ch][:].rearrange("p (c u e) -> p c u e", u=2, e=2),
+                x_raw[n, ch][:].rearrange("p (e u) c -> p c u e", u=2),
+            )
+
+        def quantize_x(n, ch):
+            if n not in x_codes:
+                x_codes[n] = codes_and_scales(keep, C, "x_codes", "x_codes%d" % n, 1)
+            quantize(*x_codes[n], slice(BANK * ch, BANK * (ch + 1)), x_side[n, ch][:], E4M3)
+
+        def interleave(engine, out, in_):
+            copy_on(
+                engine,
+                out.rearrange("p (c i j) -> p c j i", i=4, j=4),
+                in_.rearrange("p j (c i) -> p c j i", i=4),
+            )
+
+        def interleave_v(h, ch, engine):
+            v_side[h, ch] = work.tile([P, 4 * BANK], BF16, name="v_side", tag="v_side", align_bytes=64)
+            interleave(engine, v_side[h, ch][:], v_raw[h][:, :, BANK * ch : BANK * (ch + 1)])
+
+        def quantize_v(h, ch):
+            if h not in v_codes:
+                v_codes[h] = codes_and_scales(keep, C, "v_codes", "v_codes%d" % h, 1)
+            quantize(*v_codes[h], slice(BANK * ch, BANK * (ch + 1)), v_side[h, ch][:], E4M3)
+
+        def multiply(key, passes):
+            out = take_bank(key)
+            for i, (left, left_fmt, left_cols, right, right_fmt, right_cols) in enumerate(passes):
+                nc.tensor.matmul_mx(
+                    out=out[:],
+                    lhsT=left[0][:, left_cols].bitcast(left_fmt),
+                    lhsT_scale=left[1][:, left_cols],
+                    rhs=right[0][:, right_cols].bitcast(right_fmt),
+                    rhs_scale=right[1][:, right_cols],
+                    start=(i == 0),
+                    stop=(i == len(passes) - 1),
+                )
+
+        dz = {}
+
+        def make_dz(step, b, engines):
+            n, h = step
+            for i in range(2):
+                multiply(
+                    ("dh", step, 2 * b + i),
+                    [
+                        (
+                            keys_codes[step, b],
+                            E4M3,
+                            slice(256 * g + 128 * i, 256 * g + 128 * (i + 1)),
+                            grad_codes[n],
+                            E5M2,
+                            slice(BANK * g, BANK * (g + 1)),
+                        )
+                        for g in range(2)
+                    ],
+                )
+            if step not in dz:
+                dz[step] = keep.tile([P, 4, TQ], BF16, name="dz", tag="dz%d%d" % step, align_bytes=64)
+            for i in range(2):
+                j = 2 * b + i
+                out = dz[step][:, j, :].rearrange("p (u q e) -> p u q e", u=2, e=2)
+                in_ = bank_of(("dh", step, j))[:].rearrange("p (e u q) -> p u q e", u=2, e=2)
+                scale = dz_scale[:, h, j : j + 1]
+                if engines[i] == "V":
+                    nc.vector.tensor_scalar(out=out, in0=in_, scalar1=scale, scalar2=None, op0=MULT)
+                else:
+                    nc.scalar.activation(out=out, in_=in_, func=COPY, scale=scale)
+                give_bank(("dh", step, j))
+
+        token_side, token_codes = {}, {}
+
+        def turn_dz(step, engines):
+            for b in range(2):
+                transpose_words(
+                    ("turn", step, b),
+                    [dz[step][:, 2 * b + i, :] for i in range(2)],
+                    [slice(128 * u, 128 * (u + 1)) for u in range(2)],
+                )
+            token_side[step] = work.tile([P, 4 * BANK], BF16, name="token_side", tag="token_side", align_bytes=64)
+            for b in range(2):
+                copy_words(("turn", step, b), token_side[step][:, 1024 * b : 1024 * (b + 1)], engines[b])
+
+        def quantize_dz_tokens(step):
+            token_codes[step] = codes_and_scales(keep, BANK, "token_codes", "token_codes%d%d" % step, 1)
+            quantize(*token_codes[step], slice(0, BANK), token_side[step][:], E5M2)
+
+        embed_side, embed_codes = {}, {}
+
+        def interleave_dz(step, u, engine):
+            if step not in embed_side:
+                embed_side[step] = work.tile([P, 4 * TQ], BF16, name="embed_side", tag="embed_side", align_bytes=64)
+            interleave(engine, embed_side[step][:, 1024 * u : 1024 * (u + 1)], dz[step][:, :, 256 * u : 256 * (u + 1)])
+
+        def quantize_dz_embed(step):
+            embed_codes[step] = codes_and_scales(keep, TQ, "embed_codes", "embed_codes%d%d" % step, 1)
+            quantize(*embed_codes[step], slice(0, TQ), embed_side[step][:], E5M2)
+
+        d_out, dot, factor = {}, {}, {}
+
+        def d_matmul(h, j):
+            for ch in range(2):
+                multiply(
+                    ("d", h, j, ch),
+                    [
+                        (
+                            token_codes[n, h],
+                            E5M2,
+                            slice(128 * j, 128 * (j + 1)),
+                            x_codes[n],
+                            E4M3,
+                            slice(BANK * ch, BANK * (ch + 1)),
+                        )
+                        for n in range(N)
+                    ],
+                )
+
+        def d_dot(h, j):
+            d_out[h, j] = raw.tile([P, C], F32, name="d_out", tag="%s%d%d" % (("x", "keys")[h], j // 2, j % 2))
+            dot[h, j] = work.tile([P, 2], F32, name="dot", tag="dot", bufs=3)
+            for ch in range(2):
+                cols = slice(BANK * ch, BANK * (ch + 1))
+                nc.vector.scalar_tensor_tensor(
+                    out=d_out[h, j][:, cols],
+                    in0=bank_of(("d", h, j, ch))[:],
+                    scalar=1.0,
+                    in1=v_raw[h][:, j, cols],
+                    op0=MULT,
+                    op1=MULT,
+                    accum_out=dot[h, j][:, ch : ch + 1],
+                )
+
+        def d_factor(h, j):
+            factor[h, j] = work.tile([P, 1], F32, name="factor", tag="factor", bufs=3)
             nc.vector.tensor_scalar(
-                out=coef[G, t][:],
-                in0=acc[G, t][:, 0:1],
-                scalar1=acc[G, t][:, 1:2],
-                scalar2=neg_r2[:, G, t : t + 1],
+                out=factor[h, j][:],
+                in0=dot[h, j][:, 0:1],
+                scalar1=dot[h, j][:, 1:2],
+                scalar2=minus_r2[:, h, j : j + 1],
                 op0=ADD,
                 op1=MULT,
             )
 
-        def fb(G, t, ch):
-            cols = slice(512 * ch, 512 * (ch + 1))
-            nc.vector.scalar_tensor_tensor(
-                out=dv[G, t][:, cols],
-                in0=v_raw[G][:, t, cols],
-                scalar=coef[G, t][:],
-                in1=psb["d", G, t, ch][:],
-                op0=MULT,
-                op1=ADD,
-            )
-
-        def store_d(G, t, c0=0, c1=C):
-            dst = out_1[512 * G : 512 * (G + 1), :].rearrange("(p j) c -> p j c", j=4)
-            nc.sync.dma_start(out=dst[:, t, c0:c1], in_=dv[G, t][:, c0:c1])
-
-        ox = {}
-
-        def dx(n, j, ch, b):
-            pt = bank(b)
-            psb["x", n, j, ch] = pt
-            rows = slice(128 * j, 128 * (j + 1))
-            cols = slice(512 * ch, 512 * (ch + 1))
-            for G in range(2):
-                nc.tensor.matmul_mx(
-                    out=pt[:],
-                    lhsT=ze_codes[n, G][:, rows].bitcast(E5M2),
-                    lhsT_scale=ze_scl[n, G][:, rows],
-                    rhs=v_codes[G][:, cols].bitcast(E4M3),
-                    rhs_scale=v_scl[G][:, cols],
-                    start=(G == 0),
-                    stop=(G == 1),
+        def d_finish(h, j, store_halves=False):
+            dst = out_1[512 * h : 512 * (h + 1), :].rearrange("(p j) c -> p j c", j=4)
+            for ch in range(2):
+                cols = slice(BANK * ch, BANK * (ch + 1))
+                nc.vector.scalar_tensor_tensor(
+                    out=d_out[h, j][:, cols],
+                    in0=v_raw[h][:, j, cols],
+                    scalar=factor[h, j][:],
+                    in1=bank_of(("d", h, j, ch))[:],
+                    op0=MULT,
+                    op1=ADD,
                 )
+                give_bank(("d", h, j, ch))
+                if store_halves:
+                    nc.sync.dma_start(out=dst[:, j, cols], in_=d_out[h, j][:, cols])
+            if not store_halves:
+                nc.sync.dma_start(out=dst[:, j, :], in_=d_out[h, j][:])
 
-        def ex(n, j, ch, eng):
-            ox[n, j, ch] = outs.tile([P, 512], F32, name="ox", tag="ox", bufs=4)
-            copy(eng, ox[n, j, ch][:], psb["x", n, j, ch][:])
+        dx_out = {}
 
-        def store_x(n, j, ch):
-            dst = out_0[n, :, :].rearrange("(q j) c -> q j c", j=4)
-            nc.sync.dma_start(out=dst[:, j, 512 * ch : 512 * (ch + 1)], in_=ox[n, j, ch][:])
+        def dx(n, u, ch, engines):
+            cols = slice(BANK * ch, BANK * (ch + 1))
+            for b in range(2):
+                rows = slice(256 * u + 128 * b, 256 * u + 128 * (b + 1))
+                multiply(
+                    ("dx", n, u, b, ch), [(embed_codes[n, h], E5M2, rows, v_codes[h], E4M3, cols) for h in range(2)]
+                )
+            if (n, u) not in dx_out:
+                if n == 0:
+                    dx_out[n, u] = raw.tile([P, 2, C], F32, name="dx_out", tag="grad%d" % u)
+                else:
+                    dx_out[n, u] = work.tile([P, 2, C], F32, name="dx_out", tag="grad_side", align_bytes=64)
+            for b in range(2):
+                copy_on(engines[b], dx_out[n, u][:, b, cols], bank_of(("dx", n, u, b, ch))[:])
+                give_bank(("dx", n, u, b, ch))
+            if ch == 1:
+                dst = out_0[n, :, :].rearrange("(b m u) c -> m b u c", b=2, u=2)
+                for b in range(2):
+                    nc.sync.dma_start(out=dst[:, b, u, :], in_=dx_out[n, u][:, b, :])
 
-        def dx_half(i, ch):
-            dx(XT[i][0], XT[i][1], ch, "t")
-            ex(XT[i][0], XT[i][1], ch, "s")
-            if (i, ch) != (0, 0):
-                store_x(XT[(i - 1) % 8][0], XT[(i - 1) % 8][1], ch if i > 0 else 0)
 
-        TILES = [(G, t) for G in range(2) for t in range(4)]
-        XT = [(n, j) for n in range(2) for j in range(4)]
-        STEPS = [S00, S01, S10, S11]
-        X_HALF = [(0, 0), (0, 1), (1, 0), (1, 1)]
+        transpose_grad(0, 0, "VV")
+        transpose_grad(1, 0, "VV")
+        transpose_keys(S00, 0, "VS")
+        transpose_grad(1, 1, "SS")
+        quantize_keys(S00, 0)
+        quantize_grad(1, 0)
+        transpose_grad(0, 1, "VV")
+        interleave_x(1, 0, "S")
+        quantize_grad(0, 0)
+        quantize_grad(0, 1)
+        quantize_grad(1, 1)
+        transpose_keys(S01, 0, "VS")
+        quantize_keys(S01, 0)
+        transpose_keys(S00, 1, "SS")
+        interleave_v(0, 0, "V")
+        quantize_keys(S00, 1)
+        interleave_v(0, 1, "S")
+        make_factors()
 
-        def pair_tk(s, th):
-            tk(s, th, 0, "t")
-            tk(s, th, 1, "t")
-            ek(s, th, 0, "s")
-            ek(s, th, 1, "s")
+        make_dz(S00, 0, "SV")
+        transpose_keys(S10, 0, "SS")
+        quantize_v(0, 0)
+        interleave_x(0, 0, "V")
+        quantize_keys(S10, 0)
+        quantize_v(0, 1)
+        quantize_x(0, 0)
+        make_dz(S00, 1, "SS")
+        transpose_keys(S10, 1, "SS")
+        quantize_x(1, 0)
+        quantize_keys(S10, 1)
+        make_dz(S01, 0, "SS")
+        interleave_dz(S00, 0, "S")
+        interleave_dz(S00, 1, "V")
+        make_dz(S10, 0, "SV")
+        make_dz(S10, 1, "VS")
+        quantize_dz_embed(S00)
+        interleave_x(0, 1, "V")
+        transpose_keys(S01, 1, "SV")
+        turn_dz(S00, "SV")
+        turn_dz(S10, "SS")
+        transpose_keys(S11, 0, "SS")
+        quantize_keys(S01, 1)
+        quantize_dz_tokens(S10)
+        quantize_dz_tokens(S00)
+        interleave_x(1, 1, "S")
+        quantize_keys(S11, 0)
+        make_dz(S01, 1, "VV")
+        quantize_x(0, 1)
+        quantize_x(1, 1)
+        interleave_v(1, 0, "V")
+        interleave_dz(S01, 0, "V")
+        make_dz(S11, 0, "SS")
+        transpose_keys(S11, 1, "SS")
 
-        def pair_mm(s, a):
-            mm(s, a, "m")
-            mm(s, a + 1, "m")
-            eh(s, a, "s")
-            eh(s, a + 1, "s")
+        d_matmul(0, 0)
+        interleave_dz(S01, 1, "S")
+        d_dot(0, 0)
+        quantize_keys(S11, 1)
+        d_matmul(0, 1)
+        quantize_dz_embed(S01)
+        d_factor(0, 0)
+        interleave_v(1, 1, "S")
+        make_dz(S11, 1, "SS")
+        quantize_v(1, 0)
+        d_finish(0, 0)
+        d_dot(0, 1)
+        dx(0, 0, 0, "SS")
+        turn_dz(S11, "SS")
+        dx(0, 1, 0, "SS")
+        interleave_dz(S11, 0, "V")
+        turn_dz(S01, "SS")
+        d_factor(0, 1)
+        quantize_v(1, 1)
+        d_finish(0, 1)
+        interleave_dz(S10, 0, "V")
+        interleave_dz(S11, 1, "S")
+        quantize_dz_tokens(S11)
+        dx(0, 0, 1, "SS")
+        d_matmul(0, 2)
+        quantize_dz_tokens(S01)
+        dx(0, 1, 1, "SS")
+        interleave_dz(S10, 1, "V")
+        quantize_dz_embed(S11)
+        quantize_dz_embed(S10)
 
-        def pair_tg(n, bh, e0, e1):
-            tg(n, bh, 0, "t")
-            tg(n, bh, 1, "t")
-            eg(n, bh, 0, e0)
-            eg(n, bh, 1, e1)
-
-        def pair_tz(s):
-            tz(s, 0, "t")
-            tz(s, 1, "t")
-            ez(s, 0, "s")
-            ez(s, 1, "s")
-
-        make_constants()
-        pair_tg(0, 0, "s", "v")
-        pair_tg(0, 1, "s", "v")
-        qg(0, 0)
-        qg(0, 1)
-        pair_tk(S00, 0)
-        qk(S00, 0)
-        ix(0, 0, "v")
-        pair_tk(S00, 1)
-        qk(S00, 1)
-        qx(0, 0)
-        for k in range(4):
-            s = STEPS[k]
-            if k < 3:
-                pair_tk(STEPS[k + 1], 0)
-                qk(STEPS[k + 1], 0)
-            if k > 0:
-                pair_tz(STEPS[k - 1])
-                iz(STEPS[k - 1], 0, "v")
-                iz(STEPS[k - 1], 1, "v")
-                qz(STEPS[k - 1])
-                qe(STEPS[k - 1])
-            if k == 1:
-                pair_tg(1, 0, "s", "v")
-            pair_mm(s, 0)
-            if k < 3:
-                ix(X_HALF[k + 1][0], X_HALF[k + 1][1], "v")
-                pair_tk(STEPS[k + 1], 1)
-                qk(STEPS[k + 1], 1)
-                qx(X_HALF[k + 1][0], X_HALF[k + 1][1])
-            if k == 1:
-                pair_tg(1, 1, "s", "v")
-                qg(1, 0)
-                qg(1, 1)
-            if k == 3:
-                iv(0, 0, "s", (0, 256))
-            pair_mm(s, 2)
-
-        d(0, 0, 0, "m")
-        d(0, 0, 1, "m")
-        pair_tz(S11)
-        d(0, 1, 0, "m")
-        fa(0, 0, 0)
-        fa(0, 0, 1)
-        iz(S11, 0, "v")
-        fc(0, 0)
-        iz(S11, 1, "v")
-        iv(0, 0, "s", (256, 512))
-        iv(1, 0, "s")
-        qz(S11)
-        qe(S11)
-        qv(0, 0)
-        iv(0, 1, "s")
-        XQ = {1: [(0, 0), (1, 0)], 2: [(2, 0), (3, 0), (4, 0)], 3: [(5, 0), (6, 0), (7, 0)], 4: [(0, 1), (1, 1), (2, 1)], 5: [(3, 1), (4, 1), (5, 1)], 6: [(6, 1), (7, 1)]}
-        for i in range(8):
-            G, t = TILES[i]
-            if i < 7:
-                G1, t1 = TILES[i + 1]
-                fa(G1, t1, 0)
-                if i == 1:
-                    qv(1, 0)
-                if i == 2:
-                    qv(0, 1)
-                if i == 4:
-                    qv(1, 1)
-            fb(G, t, 0)
-            if i < 7:
-                d(G1, t1, 1, "m")
-                fa(G1, t1, 1)
-            fb(G, t, 1)
-            store_d(G, t)
-            if i < 6:
-                d(TILES[i + 2][0], TILES[i + 2][1], 0, "m")
-            if i < 7:
-                fc(G1, t1)
-            for q in XQ.get(i, []):
-                dx_half(q[0], q[1])
-            if i == 2:
-                iv(1, 1, "s")
-        store_x(1, 3, 1)
+        d_matmul(0, 3)
+        dx(1, 0, 0, "SS")
+        for first, second, after, dx_after in (
+            ((0, 2), (0, 3), ((1, 0), (1, 1)), ((1, 0), (0, 1))),
+            ((1, 0), (1, 1), ((1, 2), (1, 3)), ((1, 1),)),
+            ((1, 2), (1, 3), (), ()),
+        ):
+            last = not after
+            d_dot(*first)
+            d_dot(*second)
+            d_factor(*first)
+            d_factor(*second)
+            d_finish(*first)
+            if not last:
+                d_matmul(*after[0])
+            d_finish(*second, store_halves=last)
+            if not last:
+                d_matmul(*after[1])
+            for u, ch in dx_after:
+                dx(1, u, ch, "SS")

from contextlib import ExitStack
import math

import concourse.mybir as mybir
from concourse.masks import make_identity

N, TQ, TS, C, E = 2, 512, 1024, 1024, 1024
TOKENS = N * TQ

FLOPS = 2 * TOKENS * (TS * E + E * C + E * C)
BYTES = 2 * (N * TQ * C + N * E * TS + E * C + E + N * TQ * TS) + 4 * E + 4 * (TOKENS * C + E * C)

F32 = mybir.dt.float32
BF16 = mybir.dt.bfloat16
U32 = mybir.dt.uint32
U8 = mybir.dt.uint8
E4M3 = mybir.dt.float8_e4m3fn_x4
E5M2 = mybir.dt.float8_e5m2_x4
MULT = mybir.AluOpType.mult
ADD = mybir.AluOpType.add
COPY = mybir.ActivationFunctionType.Copy

P = 128
BANK = 512
SQRT_HALF = math.sqrt(0.5)

S00, S01, S10, S11 = (0, 0), (0, 1), (1, 0), (1, 1)


def tile_attentionlayer_pa_v_kernel(
    tc, x, target_embedding, encoder_keys, in_proj_v, in_proj_g, in_proj_b, v_rnorm, grad_out, out_0, out_1
):
    nc = tc.nc

    with ExitStack() as ctx:
        raw = ctx.enter_context(tc.tile_pool(name="raw", bufs=1))
        work = ctx.enter_context(tc.tile_pool(name="work", bufs=2))
        keep = ctx.enter_context(tc.tile_pool(name="keep", bufs=1))
        psum = ctx.enter_context(tc.psum_pool(name="psum", bufs=1))
        ctx.enter_context(tc.manual_schedule())

        free_banks = list(range(8))
        banks = {}

        def take_bank(key):
            b = free_banks[0]
            free_banks.remove(b)
            banks[key] = (b, psum.tile([P, BANK], F32, name="bank", tag="bank%d" % b))
            return banks[key][1]

        def bank_of(key):
            return banks[key][1]

        def give_bank(key):
            free_banks.append(banks[key][0])

        def copy_on(engine, out, in_):
            if engine == "V":
                nc.vector.tensor_copy(out=out, in_=in_)
            else:
                nc.scalar.copy(out=out, in_=in_)

        grad_raw = {n: raw.tile([P, 4, TS], BF16, name="grad_raw", tag="grad%d" % n) for n in range(N)}
        keys_raw = {s: raw.tile([P, 4, TS], BF16, name="keys_raw", tag="keys%d%d" % s) for s in (S00, S01, S10, S11)}
        x_raw = {s: raw.tile([P, 4, BANK], BF16, name="x_raw", tag="x%d%d" % s) for s in (S00, S01, S10, S11)}
        v_raw = {h: raw.tile([P, 4, C], BF16, name="v_raw", tag="v%d" % h) for h in range(2)}
        gain = keep.tile([P, 2, 4], BF16, name="gain")
        rnorm = keep.tile([P, 2, 4], F32, name="rnorm")

        def load_grad(n, b):
            src = grad_out[n, :, :].rearrange("(p j) k -> p j k", j=4)
            nc.sync.dma_start(out=grad_raw[n][:, 2 * b : 2 * b + 2, :], in_=src[:, 2 * b : 2 * b + 2, :])

        def load_keys(step, b):
            n, h = step
            src = encoder_keys[n, 512 * h : 512 * (h + 1), :].rearrange("(p j) k -> p j k", j=4)
            nc.sync.dma_start(out=keys_raw[step][:, 2 * b : 2 * b + 2, :], in_=src[:, 2 * b : 2 * b + 2, :])

        def load_x(n, ch):
            src = x[n, :, :].rearrange("(p j) c -> p j c", j=4)
            nc.sync.dma_start(out=x_raw[n, ch][:], in_=src[:, :, BANK * ch : BANK * (ch + 1)])

        def load_v(h):
            nc.sync.dma_start(
                out=v_raw[h][:], in_=in_proj_v[512 * h : 512 * (h + 1), :].rearrange("(p j) c -> p j c", j=4)
            )

        def load_vectors():
            nc.sync.dma_start(out=gain[:], in_=in_proj_g.rearrange("(h p j) -> p h j", h=2, j=4))
            nc.sync.dma_start(out=rnorm[:], in_=v_rnorm.rearrange("(h p j) -> p h j", h=2, j=4))

        load_grad(0, 0)
        load_grad(1, 0)
        load_keys(S00, 0)
        load_grad(1, 1)
        load_grad(0, 1)
        load_x(1, 0)
        load_vectors()
        load_keys(S01, 0)
        load_keys(S00, 1)
        load_v(0)
        load_keys(S10, 0)
        load_x(0, 0)
        load_keys(S10, 1)
        load_x(0, 1)
        load_keys(S01, 1)
        load_x(1, 1)
        load_v(1)
        load_keys(S11, 0)
        load_keys(S11, 1)

        ident = keep.tile([P, P], F32, name="ident")
        make_identity(nc, ident[:])
        dz_scale = keep.tile([P, 2, 4], F32, name="dz_scale")
        minus_r2 = keep.tile([P, 2, 4], F32, name="minus_r2")

        def make_factors():
            nc.vector.scalar_tensor_tensor(
                out=dz_scale[:], in0=gain[:], scalar=SQRT_HALF, in1=rnorm[:], op0=MULT, op1=MULT
            )
            nc.vector.scalar_tensor_tensor(
                out=minus_r2[:], in0=rnorm[:], scalar=-1.0, in1=rnorm[:], op0=MULT, op1=MULT
            )

        def codes_and_scales(pool, width, name, tag, bufs):
            codes = pool.tile([P, width], U32, name=name, tag=tag, bufs=bufs, align_bytes=64)
            scales = pool.tile([P, width], U8, name=name + "_scales", tag=tag + "_scales", bufs=bufs, align_bytes=64)
            return codes, scales

        def quantize(codes, scales, cols, in_, fmt):
            nc.vector.quantize_mx(out=codes[:, cols].bitcast(fmt), scales=scales[:, cols], in_=in_)

        def transpose_words(key, row_tiles, runs):
            pt = take_bank(key)
            for i in range(2):
                words = row_tiles[i].bitcast(F32)
                for u in range(2):
                    nc.tensor.transpose(
                        pt[:, 256 * u + 128 * i : 256 * u + 128 * (i + 1)], words[:, runs[u]], ident[:]
                    )

        def copy_words(key, out, engine):
            copy_on(
                engine,
                out.bitcast(F32).rearrange("p (r u) -> p r u", u=2),
                bank_of(key)[:].rearrange("p (u r) -> p r u", u=2),
            )
            give_bank(key)

        def position_runs(g):
            return [slice(256 * g + u, 256 * (g + 1), 2) for u in range(2)]

        grad_side, grad_codes = {}, {}

        def transpose_grad(n, b, engines):
            for g in range(2):
                transpose_words(("grad", n, b, g), [grad_raw[n][:, 2 * b + i, :] for i in range(2)], position_runs(g))
            if n not in grad_side:
                grad_side[n] = work.tile([P, 2, 4 * BANK], BF16, name="grad_side", tag="grad_side", align_bytes=64)
            for g in range(2):
                copy_words(("grad", n, b, g), grad_side[n][:, g, 1024 * b : 1024 * (b + 1)], engines[g])

        def quantize_grad(n, g):
            if n not in grad_codes:
                grad_codes[n] = codes_and_scales(keep, 2 * BANK, "grad_codes", "grad_codes%d" % n, 1)
            quantize(*grad_codes[n], slice(BANK * g, BANK * (g + 1)), grad_side[n][:, g, :], E5M2)

        keys_side, keys_codes = {}, {}

        def transpose_keys(step, b, engines):
            for g in range(2):
                transpose_words(
                    ("keys", step, b, g), [keys_raw[step][:, 2 * b + i, :] for i in range(2)], position_runs(g)
                )
            keys_side[step, b] = work.tile([P, 4 * BANK], BF16, name="keys_side", tag="keys_side", bufs=4, align_bytes=64)
            for g in range(2):
                copy_words(("keys", step, b, g), keys_side[step, b][:, 1024 * g : 1024 * (g + 1)], engines[g])

        def quantize_keys(step, b):
            keys_codes[step, b] = codes_and_scales(work, BANK, "keys_codes", "keys_codes", 6)
            quantize(*keys_codes[step, b], slice(0, BANK), keys_side[step, b][:], E4M3)

        x_side, x_codes, v_side, v_codes = {}, {}, {}, {}

        def interleave_x(n, ch, engine):
            x_side[n, ch] = work.tile([P, 4 * BANK], BF16, name="x_side", tag="x_side", align_bytes=64)
            copy_on(
                engine,
                x_side[n, ch][:].rearrange("p (c u e) -> p c u e", u=2, e=2),
                x_raw[n, ch][:].rearrange("p (e u) c -> p c u e", u=2),
            )

        def quantize_x(n, ch):
            if n not in x_codes:
                x_codes[n] = codes_and_scales(keep, C, "x_codes", "x_codes%d" % n, 1)
            quantize(*x_codes[n], slice(BANK * ch, BANK * (ch + 1)), x_side[n, ch][:], E4M3)

        def interleave(engine, out, in_):
            copy_on(
                engine,
                out.rearrange("p (c i j) -> p c j i", i=4, j=4),
                in_.rearrange("p j (c i) -> p c j i", i=4),
            )

        def interleave_v(h, ch, engine):
            v_side[h, ch] = work.tile([P, 4 * BANK], BF16, name="v_side", tag="v_side", align_bytes=64)
            interleave(engine, v_side[h, ch][:], v_raw[h][:, :, BANK * ch : BANK * (ch + 1)])

        def quantize_v(h, ch):
            if h not in v_codes:
                v_codes[h] = codes_and_scales(keep, C, "v_codes", "v_codes%d" % h, 1)
            quantize(*v_codes[h], slice(BANK * ch, BANK * (ch + 1)), v_side[h, ch][:], E4M3)

        def multiply(key, passes):
            out = take_bank(key)
            for i, (left, left_fmt, left_cols, right, right_fmt, right_cols) in enumerate(passes):
                nc.tensor.matmul_mx(
                    out=out[:],
                    lhsT=left[0][:, left_cols].bitcast(left_fmt),
                    lhsT_scale=left[1][:, left_cols],
                    rhs=right[0][:, right_cols].bitcast(right_fmt),
                    rhs_scale=right[1][:, right_cols],
                    start=(i == 0),
                    stop=(i == len(passes) - 1),
                )

        dz = {}

        def make_dz(step, b, engines):
            n, h = step
            for i in range(2):
                multiply(
                    ("dh", step, 2 * b + i),
                    [
                        (
                            keys_codes[step, b],
                            E4M3,
                            slice(256 * g + 128 * i, 256 * g + 128 * (i + 1)),
                            grad_codes[n],
                            E5M2,
                            slice(BANK * g, BANK * (g + 1)),
                        )
                        for g in range(2)
                    ],
                )
            if step not in dz:
                dz[step] = keep.tile([P, 4, TQ], BF16, name="dz", tag="dz%d%d" % step, align_bytes=64)
            for i in range(2):
                j = 2 * b + i
                out = dz[step][:, j, :].rearrange("p (u q e) -> p u q e", u=2, e=2)
                in_ = bank_of(("dh", step, j))[:].rearrange("p (e u q) -> p u q e", u=2, e=2)
                scale = dz_scale[:, h, j : j + 1]
                if engines[i] == "V":
                    nc.vector.tensor_scalar(out=out, in0=in_, scalar1=scale, scalar2=None, op0=MULT)
                else:
                    nc.scalar.activation(out=out, in_=in_, func=COPY, scale=scale)
                give_bank(("dh", step, j))

        token_side, token_codes = {}, {}

        def turn_dz(step, engines):
            for b in range(2):
                transpose_words(
                    ("turn", step, b),
                    [dz[step][:, 2 * b + i, :] for i in range(2)],
                    [slice(128 * u, 128 * (u + 1)) for u in range(2)],
                )
            token_side[step] = work.tile([P, 4 * BANK], BF16, name="token_side", tag="token_side", align_bytes=64)
            for b in range(2):
                copy_words(("turn", step, b), token_side[step][:, 1024 * b : 1024 * (b + 1)], engines[b])

        def quantize_dz_tokens(step):
            token_codes[step] = codes_and_scales(keep, BANK, "token_codes", "token_codes%d%d" % step, 1)
            quantize(*token_codes[step], slice(0, BANK), token_side[step][:], E5M2)

        embed_side, embed_codes = {}, {}

        def interleave_dz(step, u, engine):
            if step not in embed_side:
                embed_side[step] = work.tile([P, 4 * TQ], BF16, name="embed_side", tag="embed_side", align_bytes=64)
            interleave(engine, embed_side[step][:, 1024 * u : 1024 * (u + 1)], dz[step][:, :, 256 * u : 256 * (u + 1)])

        def quantize_dz_embed(step):
            embed_codes[step] = codes_and_scales(keep, TQ, "embed_codes", "embed_codes%d%d" % step, 1)
            quantize(*embed_codes[step], slice(0, TQ), embed_side[step][:], E5M2)

        d_out, dot, factor = {}, {}, {}

        def d_matmul(h, j):
            for ch in range(2):
                multiply(
                    ("d", h, j, ch),
                    [
                        (
                            token_codes[n, h],
                            E5M2,
                            slice(128 * j, 128 * (j + 1)),
                            x_codes[n],
                            E4M3,
                            slice(BANK * ch, BANK * (ch + 1)),
                        )
                        for n in range(N)
                    ],
                )

        def d_dot(h, j):
            d_out[h, j] = raw.tile([P, C], F32, name="d_out", tag="%s%d%d" % (("x", "keys")[h], j // 2, j % 2))
            dot[h, j] = work.tile([P, 2], F32, name="dot", tag="dot", bufs=3)
            for ch in range(2):
                cols = slice(BANK * ch, BANK * (ch + 1))
                nc.vector.scalar_tensor_tensor(
                    out=d_out[h, j][:, cols],
                    in0=bank_of(("d", h, j, ch))[:],
                    scalar=1.0,
                    in1=v_raw[h][:, j, cols],
                    op0=MULT,
                    op1=MULT,
                    accum_out=dot[h, j][:, ch : ch + 1],
                )

        def d_factor(h, j):
            factor[h, j] = work.tile([P, 1], F32, name="factor", tag="factor", bufs=3)
            nc.vector.tensor_scalar(
                out=factor[h, j][:],
                in0=dot[h, j][:, 0:1],
                scalar1=dot[h, j][:, 1:2],
                scalar2=minus_r2[:, h, j : j + 1],
                op0=ADD,
                op1=MULT,
            )

        def d_finish(h, j, store_halves=False):
            dst = out_1[512 * h : 512 * (h + 1), :].rearrange("(p j) c -> p j c", j=4)
            for ch in range(2):
                cols = slice(BANK * ch, BANK * (ch + 1))
                nc.vector.scalar_tensor_tensor(
                    out=d_out[h, j][:, cols],
                    in0=v_raw[h][:, j, cols],
                    scalar=factor[h, j][:],
                    in1=bank_of(("d", h, j, ch))[:],
                    op0=MULT,
                    op1=ADD,
                )
                give_bank(("d", h, j, ch))
                if store_halves:
                    nc.sync.dma_start(out=dst[:, j, cols], in_=d_out[h, j][:, cols])
            if not store_halves:
                nc.sync.dma_start(out=dst[:, j, :], in_=d_out[h, j][:])

        dx_out = {}

        def dx(n, u, ch, engines):
            cols = slice(BANK * ch, BANK * (ch + 1))
            for b in range(2):
                rows = slice(256 * u + 128 * b, 256 * u + 128 * (b + 1))
                multiply(
                    ("dx", n, u, b, ch), [(embed_codes[n, h], E5M2, rows, v_codes[h], E4M3, cols) for h in range(2)]
                )
            if (n, u) not in dx_out:
                if n == 0:
                    dx_out[n, u] = raw.tile([P, 2, C], F32, name="dx_out", tag="grad%d" % u)
                else:
                    dx_out[n, u] = work.tile([P, 2, C], F32, name="dx_out", tag="grad_side", align_bytes=64)
            for b in range(2):
                copy_on(engines[b], dx_out[n, u][:, b, cols], bank_of(("dx", n, u, b, ch))[:])
                give_bank(("dx", n, u, b, ch))
            if ch == 1:
                dst = out_0[n, :, :].rearrange("(b m u) c -> m b u c", b=2, u=2)
                for b in range(2):
                    nc.sync.dma_start(out=dst[:, b, u, :], in_=dx_out[n, u][:, b, :])


        transpose_grad(0, 0, "VV")
        transpose_grad(1, 0, "VV")
        transpose_keys(S00, 0, "VS")
        transpose_grad(1, 1, "SS")
        quantize_keys(S00, 0)
        quantize_grad(1, 0)
        transpose_grad(0, 1, "VV")
        interleave_x(1, 0, "S")
        quantize_grad(0, 0)
        quantize_grad(0, 1)
        quantize_grad(1, 1)
        transpose_keys(S01, 0, "VS")
        quantize_keys(S01, 0)
        transpose_keys(S00, 1, "SS")
        interleave_v(0, 0, "V")
        quantize_keys(S00, 1)
        interleave_v(0, 1, "S")
        make_factors()

        make_dz(S00, 0, "SV")
        transpose_keys(S10, 0, "SS")
        quantize_v(0, 0)
        interleave_x(0, 0, "V")
        quantize_keys(S10, 0)
        quantize_v(0, 1)
        quantize_x(0, 0)
        make_dz(S00, 1, "SS")
        transpose_keys(S10, 1, "SS")
        quantize_x(1, 0)
        quantize_keys(S10, 1)
        make_dz(S01, 0, "SS")
        interleave_dz(S00, 0, "S")
        interleave_dz(S00, 1, "V")
        make_dz(S10, 0, "SV")
        make_dz(S10, 1, "VS")
        quantize_dz_embed(S00)
        interleave_x(0, 1, "V")
        transpose_keys(S01, 1, "SV")
        turn_dz(S00, "SV")
        turn_dz(S10, "SS")
        transpose_keys(S11, 0, "SS")
        quantize_keys(S01, 1)
        quantize_dz_tokens(S10)
        quantize_dz_tokens(S00)
        interleave_x(1, 1, "S")
        quantize_keys(S11, 0)
        make_dz(S01, 1, "VV")
        quantize_x(0, 1)
        quantize_x(1, 1)
        interleave_v(1, 0, "V")
        interleave_dz(S01, 0, "V")
        make_dz(S11, 0, "SS")
        transpose_keys(S11, 1, "SS")

        d_matmul(0, 0)
        interleave_dz(S01, 1, "S")
        d_dot(0, 0)
        quantize_keys(S11, 1)
        d_matmul(0, 1)
        quantize_dz_embed(S01)
        d_factor(0, 0)
        interleave_v(1, 1, "S")
        make_dz(S11, 1, "SS")
        quantize_v(1, 0)
        d_finish(0, 0)
        d_dot(0, 1)
        dx(0, 0, 0, "SS")
        turn_dz(S11, "SS")
        dx(0, 1, 0, "SS")
        interleave_dz(S11, 0, "V")
        turn_dz(S01, "SS")
        d_factor(0, 1)
        quantize_v(1, 1)
        d_finish(0, 1)
        interleave_dz(S10, 0, "V")
        interleave_dz(S11, 1, "S")
        quantize_dz_tokens(S11)
        dx(0, 0, 1, "SS")
        d_matmul(0, 2)
        quantize_dz_tokens(S01)
        dx(0, 1, 1, "SS")
        interleave_dz(S10, 1, "V")
        quantize_dz_embed(S11)
        quantize_dz_embed(S10)

        d_matmul(0, 3)
        dx(1, 0, 0, "SS")
        for first, second, after, dx_after in (
            ((0, 2), (0, 3), ((1, 0), (1, 1)), ((1, 0), (0, 1))),
            ((1, 0), (1, 1), ((1, 2), (1, 3)), ((1, 1),)),
            ((1, 2), (1, 3), (), ()),
        ):
            last = not after
            d_dot(*first)
            d_dot(*second)
            d_factor(*first)
            d_factor(*second)
            d_finish(*first)
            if not last:
                d_matmul(*after[0])
            d_finish(*second, store_halves=last)
            if not last:
                d_matmul(*after[1])
            for u, ch in dx_after:
                dx(1, u, ch, "SS")
